import numpy as np
import ml_dtypes


BF16 = ml_dtypes.bfloat16


def bf(x):
    return np.asarray(x, np.float32).astype(BF16)


def f64(x):
    return np.asarray(x).astype(np.float64)


E2M1 = np.array([0.0, 0.5, 1.0, 1.5, 2.0, 3.0, 4.0, 6.0, -0.0, -0.5, -1.0, -1.5, -2.0, -3.0, -4.0, -6.0])


def pack_weight(w, fmt):
    k, n = w.shape
    w = f64(bf(w)).reshape(k // 32, 32, n)
    amax = np.abs(w).max(1)
    if fmt == "e4m3":
        byte = np.frexp(amax)[1] - 1 + 127 - 7
    else:
        mant, ex = np.frexp(amax / 6.0)
        byte = np.where(mant > 0.5, ex, ex - 1) + 127
    byte = np.clip(np.where(amax > 0, byte, 1), 1, 254)
    scaled = (w * np.exp2(127.0 - byte)[:, None, :]).reshape(k, n).astype(np.float32)
    by_word = np.ascontiguousarray(scaled.reshape(k // 512, 128, 4, n).transpose(0, 1, 3, 2))
    if fmt == "e4m3":
        words = by_word.astype(ml_dtypes.float8_e4m3fn).view(np.uint8)
    else:
        c = by_word.astype(ml_dtypes.float4_e2m1fn).view(np.uint8) & 0xF
        words = c[..., 0::2] | (c[..., 1::2] << 4)
    return np.ascontiguousarray(words), np.ascontiguousarray(byte.astype(np.uint8).reshape(k // 512, 16, n))


def unpack_weight(words, scales, fmt):
    g, p, n, _ = words.shape
    if fmt == "e4m3":
        vals = np.ascontiguousarray(words).view(ml_dtypes.float8_e4m3fn).astype(np.float64)
    else:
        nib = np.empty((g, p, n, 4), np.uint8)
        nib[..., 0::2] = words & 0xF
        nib[..., 1::2] = words >> 4
        vals = E2M1[nib]
    vals = vals * np.repeat(np.exp2(scales.astype(np.float64) - 127.0), 8, axis=1)[..., None]
    return vals.transpose(0, 1, 3, 2).reshape(g * 512, n)

def pack4(w):
    words, scales = pack_weight(w, "e2m1")
    return words.reshape(words.shape[0], 128, -1), scales


def unpack4(words, scales):
    return unpack_weight(words.reshape(words.shape[0], 128, -1, 2), scales, "e2m1")


def kspread(k):
    return np.exp2(np.repeat(np.random.randint(-6, 7, k // 32), 32).astype(np.float64))


B, T, D, H, KV, HD, KB = 1, 2560, 2048, 16, 4, 128, 512
QS = H * HD
KS = KV * HD
HALF = HD // 2
QKV_RMS = 1.5


def rotary(t, cos, sin):
    tr = t.reshape(t.shape[:-1] + (HALF, 2))
    t0, t1 = tr[..., 0], tr[..., 1]
    c = cos[None, :, None, :]
    s = sin[None, :, None, :]
    o0 = t0 * c - t1 * s
    o1 = t0 * s + t1 * c
    return np.stack([o0, o1], axis=-1).reshape(t.shape)


def setup_inputs():
    s = kspread(D)
    ang = np.random.uniform(-np.pi, np.pi, (T, HALF))
    x = np.random.standard_normal((B, T, D)) * s
    x_words, x_scales = pack4(np.ascontiguousarray(x.reshape(B * T, D).T))
    w = np.random.standard_normal((QS + 2 * KS, D)) * QKV_RMS / np.sqrt(D) / s[None, :]
    words, scales = pack4(np.ascontiguousarray(w.T))
    return {"x_words": x_words,
            "x_scales": x_scales,
            "freqs_cos": bf(np.cos(ang)),
            "freqs_sin": bf(np.sin(ang)),
            "w_qkv_words": words,
            "w_qkv_scales": scales}


def reference(x_words, x_scales, freqs_cos, freqs_sin, w_qkv_words, w_qkv_scales):
    cos, sin = f64(freqs_cos), f64(freqs_sin)
    qkv = unpack4(x_words, x_scales).T.reshape(B, T, D) @ unpack4(w_qkv_words, w_qkv_scales)
    q = qkv[..., :QS].reshape(B, T, H, HD)
    k = qkv[..., QS:QS + KS].reshape(B, T, KV, HD)
    v = qkv[..., QS + KS:].reshape(B, T, KV, HD)
    q = rotary(q, cos, sin)
    k = rotary(k, cos, sin)
    return q.transpose(0, 2, 1, 3), k.transpose(0, 2, 1, 3), v.transpose(0, 2, 1, 3)

@@ -1,0 +1,220 @@
+from contextlib import ExitStack
+
+import concourse.mybir as mybir
+
+F32 = mybir.dt.float32
+BF16 = mybir.dt.bfloat16
+I32 = mybir.dt.int32
+U8 = mybir.dt.uint8
+FP4X4 = mybir.dt.float4_e2m1fn_x4
+MULT = mybir.AluOpType.mult
+ADD = mybir.AluOpType.add
+
+T, D = 2560, 2048
+H, KV, HD = 16, 4, 128
+HALF = HD // 2
+N_ALL = (H + 2 * KV) * HD
+P = 128
+PASSES = D // 512
+UNITS = T // P
+BLK = 512
+HEADS_BLK = BLK // HD
+QK_BLOCKS = (H + KV) * HD // BLK
+V_BLOCK = QK_BLOCKS
+Q_BLOCKS = H * HD // BLK
+
+FLOPS = 2 * T * D * N_ALL
+
+X_CODE_CHUNKS = ((0, 2), (2, 2), (4, 4), (8, 6), (14, 6))
+X_SCALE_CHUNKS = ((0, 4), (4, 16))
+W_SCALE_CHUNKS = ((0, 2), (2, 4))
+TABLE_CHUNKS = ((0, 2), (2, 18))
+HELD_V_UNITS = 4
+
+
+def chunk_lookup(chunks):
+    table = {}
+    for c, (start, count) in enumerate(chunks):
+        for k in range(count):
+            table[start + k] = (c, k)
+    return table
+
+
+def job_order():
+    jobs = []
+    for n in range(QK_BLOCKS + 1):
+        for i in (0, 1):
+            jobs.append((i, n))
+    for i in range(2, UNITS - HELD_V_UNITS):
+        for n in range(QK_BLOCKS + 1):
+            jobs.append((i, n))
+    for i in range(UNITS - HELD_V_UNITS, UNITS):
+        for n in range(QK_BLOCKS):
+            jobs.append((i, n))
+    for i in range(UNITS - HELD_V_UNITS, UNITS):
+        jobs.append((i, V_BLOCK))
+    return jobs
+
+
+def tile_fusedqkvattentionwrapper_pa_kernel(
+    tc, x_words, x_scales, freqs_cos, freqs_sin, w_qkv_words, w_qkv_scales, out_0, out_1, out_2
+):
+    nc = tc.nc
+    with ExitStack() as ctx:
+        ctx.enter_context(tc.manual_schedule())
+        keep = ctx.enter_context(tc.tile_pool(name="keep", bufs=1))
+        work = ctx.enter_context(tc.tile_pool(name="work", bufs=6))
+        vals = ctx.enter_context(tc.tile_pool(name="vals", bufs=4))
+        psum = ctx.enter_context(tc.psum_pool(name="psum", bufs=8))
+
+        xw = [keep.tile([P, PASSES, 2 * P * cnt], U8, name="xw%d" % c, align_bytes=64)
+              for c, (st, cnt) in enumerate(X_CODE_CHUNKS)]
+        xs = [keep.tile([P, PASSES, P * cnt], U8, name="xs%d" % c, align_bytes=64)
+              for c, (st, cnt) in enumerate(X_SCALE_CHUNKS)]
+        ww = [keep.tile([P, PASSES, 2 * BLK], U8, name="ww%d" % n, align_bytes=64)
+              for n in range(QK_BLOCKS + 1)]
+        ws = [keep.tile([P, PASSES, BLK * cnt], U8, name="ws%d" % c, align_bytes=64)
+              for c, (st, cnt) in enumerate(W_SCALE_CHUNKS)]
+        cos_raw = [keep.tile([P, cnt, HALF], BF16, name="cosr%d" % c) for c, (st, cnt) in enumerate(TABLE_CHUNKS)]
+        sin_raw = [keep.tile([P, cnt, HALF], BF16, name="sinr%d" % c) for c, (st, cnt) in enumerate(TABLE_CHUNKS)]
+        cos_tab = [keep.tile([P, cnt, HD], F32, name="cost%d" % c) for c, (st, cnt) in enumerate(TABLE_CHUNKS)]
+        sin_tab = [keep.tile([P, cnt, HD], F32, name="sint%d" % c) for c, (st, cnt) in enumerate(TABLE_CHUNKS)]
+
+        xw_of = chunk_lookup(X_CODE_CHUNKS)
+        xs_of = chunk_lookup(X_SCALE_CHUNKS)
+        ws_of = chunk_lookup(W_SCALE_CHUNKS)
+        tab_of = chunk_lookup(TABLE_CHUNKS)
+
+        def load_x_codes(c):
+            st, cnt = X_CODE_CHUNKS[c]
+            nc.sync.dma_start(
+                out=xw[c][:].bitcast(I32),
+                in_=x_words[:, :, 2 * P * st:2 * P * (st + cnt)].rearrange("g p n -> p g n").bitcast(I32),
+            )
+
+        def load_w_codes(n):
+            nc.sync.dma_start(
+                out=ww[n][:].bitcast(I32),
+                in_=w_qkv_words[:, :, 2 * BLK * n:2 * BLK * (n + 1)].rearrange("g p n -> p g n").bitcast(I32),
+            )
+
+        def load_scales(plane, dram, lo, hi):
+            for q in range(4):
+                nc.sync.dma_start(
+                    out=plane[32 * q:32 * q + 4, :, :].bitcast(I32),
+                    in_=dram[:, 4 * q:4 * q + 4, lo:hi].rearrange("g r n -> r g n").bitcast(I32),
+                )
+
+        def load_x_scales(c):
+            st, cnt = X_SCALE_CHUNKS[c]
+            load_scales(xs[c], x_scales, P * st, P * (st + cnt))
+
+        def load_w_scales(c):
+            st, cnt = W_SCALE_CHUNKS[c]
+            load_scales(ws[c], w_qkv_scales, BLK * st, BLK * (st + cnt))
+
+        for plane in (xs[0], ws[0], ws[1], xs[1]):
+            nc.vector.memset(plane[:].bitcast(I32), 0)
+
+        for c, (st, cnt) in enumerate(TABLE_CHUNKS):
+            rows = slice(P * st, P * (st + cnt))
+            nc.gpsimd.dma_start(out=cos_raw[c][:], in_=freqs_cos[rows, :].rearrange("(i p) j -> p i j", p=P))
+            nc.gpsimd.dma_start(out=sin_raw[c][:], in_=freqs_sin[rows, :].rearrange("(i p) j -> p i j", p=P))
+
+        load_x_codes(0)
+        load_w_codes(0)
+        load_x_scales(0)
+        load_w_scales(0)
+        load_w_codes(1)
+        load_w_codes(2)
+        load_w_scales(1)
+        load_w_codes(3)
+        load_w_codes(4)
+        load_w_codes(5)
+        load_x_codes(1)
+        load_x_codes(2)
+        load_x_scales(1)
+        load_x_codes(3)
+        load_x_codes(4)
+
+        for c, (st, cnt) in enumerate(TABLE_CHUNKS):
+            flat_cos = cos_raw[c][:].rearrange("p i j -> p (i j)")
+            flat_sin = sin_raw[c][:].rearrange("p i j -> p (i j)")
+            cos_pairs = cos_tab[c][:].rearrange("p i (j t) -> p (i j) t", t=2)
+            sin_pairs = sin_tab[c][:].rearrange("p i (j t) -> p (i j) t", t=2)
+            nc.scalar.copy(out=cos_pairs, in_=flat_cos.unsqueeze(2).to_broadcast([P, cnt * HALF, 2]))
+            if c == 0:
+                nc.scalar.mul(out=sin_pairs[:, :, 0], in_=flat_sin, mul=-1.0)
+                nc.scalar.copy(out=sin_pairs[:, :, 1], in_=flat_sin)
+            else:
+                nc.gpsimd.tensor_scalar(out=sin_pairs[:, :, 0], in0=flat_sin, scalar1=-1.0, scalar2=0.0,
+                                        op0=MULT, op1=ADD)
+                nc.gpsimd.tensor_scalar(out=sin_pairs[:, :, 1], in0=flat_sin, scalar1=1.0, scalar2=0.0,
+                                        op0=MULT, op1=ADD)
+
+        def chunks_of(i):
+            if i == UNITS - 1:
+                return ((0, 3, nc.gpsimd), (3, 5, nc.vector))
+            return ((0, 3, nc.gpsimd), (3, 5, nc.gpsimd))
+
+        live = {}
+
+        def by_head(ap):
+            return ap.rearrange("p (h d) -> p h d", d=HD)
+
+        def by_pair(ap):
+            return ap.rearrange("p (h j t) -> p h j t", j=HALF, t=2)
+
+        for i, n in job_order():
+            tok = slice(P * i, P * (i + 1))
+            xc, xk = xw_of[i]
+            sc, sk = xs_of[i]
+            wc, wk = ws_of[n]
+            acc = psum.tile([P, BLK], F32, name="acc")
+            for g in range(PASSES):
+                nc.tensor.matmul_mx(
+                    out=acc[:],
+                    lhsT=xw[xc][:, g, 2 * P * xk:2 * P * (xk + 1)].bitcast(FP4X4),
+                    lhsT_scale=xs[sc][:, g, P * sk:P * (sk + 1)],
+                    rhs=ww[n][:, g, :].bitcast(FP4X4),
+                    rhs_scale=ws[wc][:, g, BLK * wk:BLK * (wk + 1)],
+                    start=(g == 0),
+                    stop=(g == PASSES - 1),
+                )
+
+            if n == V_BLOCK:
+                v_sb = vals.tile([P, BLK], F32, name="v_sb")
+                nc.scalar.copy(out=v_sb[:], in_=acc[:])
+                nc.scalar.dma_start(out=out_2[0, :, tok, :].rearrange("h p d -> p h d"), in_=by_head(v_sb[:]))
+                continue
+
+            lo, hi, adder = [ch for ch in chunks_of(i) if ch[0] <= n < ch[1]][0]
+            width = (hi - lo) * BLK
+            if n == lo:
+                a_cos = work.tile([P, width], F32, name="a_cos")
+                a_sin = work.tile([P, width], F32, name="a_sin")
+                live[i] = (a_cos, a_sin)
+            a_cos, a_sin = live[i]
+            cols = slice((n - lo) * BLK, (n - lo + 1) * BLK)
+            tcn, tk = tab_of[i]
+            shape4 = [P, HEADS_BLK, HALF, 2]
+            cos_v = cos_tab[tcn][:, tk, :].rearrange("p (j t) -> p j t", t=2).unsqueeze(1).to_broadcast(shape4)
+            sin_v = sin_tab[tcn][:, tk, :].rearrange("p (j t) -> p j t", t=2).unsqueeze(1).to_broadcast(shape4)
+            pairs = by_pair(acc[:])
+            nc.vector.tensor_tensor(out=by_pair(a_cos[:, cols]), in0=pairs, in1=cos_v, op=MULT)
+            nc.vector.tensor_tensor(out=by_pair(a_sin[:, cols]), in0=pairs[:, :, :, ::-1], in1=sin_v, op=MULT)
+
+            if n == hi - 1:
+                rot = work.tile([P, width], F32, name="rot")
+                adder.tensor_tensor(out=rot[:], in0=a_cos[:], in1=a_sin[:], op=ADD)
+                q_hi = min(hi, Q_BLOCKS)
+                if lo < q_hi:
+                    nc.sync.dma_start(
+                        out=out_0[0, HEADS_BLK * lo:HEADS_BLK * q_hi, tok, :].rearrange("h p d -> p h d"),
+                        in_=by_head(rot[:, 0:(q_hi - lo) * BLK]),
+                    )
+                if hi > Q_BLOCKS:
+                    nc.sync.dma_start(
+                        out=out_1[0, :, tok, :].rearrange("h p d -> p h d"),
+                        in_=by_head(rot[:, (Q_BLOCKS - lo) * BLK:width]),
+                    )

@@ -26,10 +26,11 @@ Q_BLOCKS = H * HD // BLK
 FLOPS = 2 * T * D * N_ALL
 
 X_CODE_CHUNKS = ((0, 2), (2, 2), (4, 4), (8, 6), (14, 6))
-X_SCALE_CHUNKS = ((0, 4), (4, 16))
-W_SCALE_CHUNKS = ((0, 2), (2, 4))
-TABLE_CHUNKS = ((0, 2), (2, 18))
+X_SCALE_CHUNKS = ((0, 2), (2, 18))
+W_SCALE_CHUNKS = ((0, 1), (1, 2), (3, 3))
+TABLE_CHUNKS = ((0, 2), (2, 4), (6, 14))
 HELD_V_UNITS = 4
+WARM_MATMULS = 16
 
 
 def chunk_lookup(chunks):
@@ -63,7 +64,7 @@ def tile_fusedqkvattentionwrapper_pa_kernel(
     with ExitStack() as ctx:
         ctx.enter_context(tc.manual_schedule())
         keep = ctx.enter_context(tc.tile_pool(name="keep", bufs=1))
-        work = ctx.enter_context(tc.tile_pool(name="work", bufs=6))
+        work = ctx.enter_context(tc.tile_pool(name="work", bufs=4))
         vals = ctx.enter_context(tc.tile_pool(name="vals", bufs=4))
         psum = ctx.enter_context(tc.psum_pool(name="psum", bufs=8))
 
@@ -113,51 +114,80 @@ def tile_fusedqkvattentionwrapper_pa_kernel(
             st, cnt = W_SCALE_CHUNKS[c]
             load_scales(ws[c], w_qkv_scales, BLK * st, BLK * (st + cnt))
 
-        for plane in (xs[0], ws[0], ws[1], xs[1]):
+        def load_angles(c, queue):
+            st, cnt = TABLE_CHUNKS[c]
+            rows = slice(P * st, P * (st + cnt))
+            queue.dma_start(out=cos_raw[c][:], in_=freqs_cos[rows, :].rearrange("(i p) j -> p i j", p=P))
+            queue.dma_start(out=sin_raw[c][:], in_=freqs_sin[rows, :].rearrange("(i p) j -> p i j", p=P))
+
+        warm = keep.tile([P, P + BLK], BF16, name="warm")
+        nc.gpsimd.memset(warm[:], 0.0)
+        for plane in (xs[0], ws[0], ws[1], ws[2], xs[1]):
             nc.vector.memset(plane[:].bitcast(I32), 0)
 
-        for c, (st, cnt) in enumerate(TABLE_CHUNKS):
-            rows = slice(P * st, P * (st + cnt))
-            nc.gpsimd.dma_start(out=cos_raw[c][:], in_=freqs_cos[rows, :].rearrange("(i p) j -> p i j", p=P))
-            nc.gpsimd.dma_start(out=sin_raw[c][:], in_=freqs_sin[rows, :].rearrange("(i p) j -> p i j", p=P))
-
+        load_angles(0, nc.gpsimd)
         load_x_codes(0)
         load_w_codes(0)
         load_x_scales(0)
         load_w_scales(0)
         load_w_codes(1)
-        load_w_codes(2)
         load_w_scales(1)
+        load_w_codes(2)
         load_w_codes(3)
+        load_w_scales(2)
         load_w_codes(4)
         load_w_codes(5)
+        load_angles(1, nc.sync)
         load_x_codes(1)
-        load_x_codes(2)
         load_x_scales(1)
+        load_x_codes(2)
+        load_angles(2, nc.sync)
         load_x_codes(3)
         load_x_codes(4)
 
-        for c, (st, cnt) in enumerate(TABLE_CHUNKS):
+        warm_acc = psum.tile([P, BLK], F32, name="acc")
+        for k in range(WARM_MATMULS):
+            nc.tensor.matmul(out=warm_acc[:], lhsT=warm[:, 0:P], rhs=warm[:, P:P + BLK], start=True, stop=True)
+
+        def build_tables(c):
+            st, cnt = TABLE_CHUNKS[c]
             flat_cos = cos_raw[c][:].rearrange("p i j -> p (i j)")
             flat_sin = sin_raw[c][:].rearrange("p i j -> p (i j)")
             cos_pairs = cos_tab[c][:].rearrange("p i (j t) -> p (i j) t", t=2)
             sin_pairs = sin_tab[c][:].rearrange("p i (j t) -> p (i j) t", t=2)
             nc.scalar.copy(out=cos_pairs, in_=flat_cos.unsqueeze(2).to_broadcast([P, cnt * HALF, 2]))
-            if c == 0:
-                nc.scalar.mul(out=sin_pairs[:, :, 0], in_=flat_sin, mul=-1.0)
-                nc.scalar.copy(out=sin_pairs[:, :, 1], in_=flat_sin)
-            else:
-                nc.gpsimd.tensor_scalar(out=sin_pairs[:, :, 0], in0=flat_sin, scalar1=-1.0, scalar2=0.0,
-                                        op0=MULT, op1=ADD)
-                nc.gpsimd.tensor_scalar(out=sin_pairs[:, :, 1], in0=flat_sin, scalar1=1.0, scalar2=0.0,
-                                        op0=MULT, op1=ADD)
+            nc.scalar.mul(out=sin_pairs[:, :, 0], in_=flat_sin, mul=-1.0)
+            nc.scalar.copy(out=sin_pairs[:, :, 1], in_=flat_sin)
+
+        build_tables(0)
+        build_tables(1)
 
         def chunks_of(i):
             if i == UNITS - 1:
-                return ((0, 3, nc.gpsimd), (3, 5, nc.vector))
-            return ((0, 3, nc.gpsimd), (3, 5, nc.gpsimd))
+                return ((0, 2, nc.vector), (2, 4, nc.vector), (4, 5, nc.vector))
+            if i < 2:
+                return ((0, 3, nc.gpsimd), (3, 5, nc.gpsimd))
+            return ((0, 5, nc.gpsimd),)
 
         live = {}
+        deferred = []
+
+        def add_and_store(i, lo, hi, adder, a_cos, a_sin):
+            tok = slice(P * i, P * (i + 1))
+            width = (hi - lo) * BLK
+            rot = work.tile([P, width], F32, name="rot")
+            adder.tensor_tensor(out=rot[:], in0=a_cos[:], in1=a_sin[:], op=ADD)
+            q_hi = min(hi, Q_BLOCKS)
+            if lo < q_hi:
+                nc.sync.dma_start(
+                    out=out_0[0, HEADS_BLK * lo:HEADS_BLK * q_hi, tok, :].rearrange("h p d -> p h d"),
+                    in_=by_head(rot[:, 0:(q_hi - lo) * BLK]),
+                )
+            if hi > Q_BLOCKS:
+                nc.sync.dma_start(
+                    out=out_1[0, :, tok, :].rearrange("h p d -> p h d"),
+                    in_=by_head(rot[:, (Q_BLOCKS - lo) * BLK:width]),
+                )
 
         def by_head(ap):
             return ap.rearrange("p (h d) -> p h d", d=HD)
@@ -186,6 +216,8 @@ def tile_fusedqkvattentionwrapper_pa_kernel(
                 v_sb = vals.tile([P, BLK], F32, name="v_sb")
                 nc.scalar.copy(out=v_sb[:], in_=acc[:])
                 nc.scalar.dma_start(out=out_2[0, :, tok, :].rearrange("h p d -> p h d"), in_=by_head(v_sb[:]))
+                if i == 1:
+                    build_tables(2)
                 continue
 
             lo, hi, adder = [ch for ch in chunks_of(i) if ch[0] <= n < ch[1]][0]
@@ -205,16 +237,10 @@ def tile_fusedqkvattentionwrapper_pa_kernel(
             nc.vector.tensor_tensor(out=by_pair(a_sin[:, cols]), in0=pairs[:, :, :, ::-1], in1=sin_v, op=MULT)
 
             if n == hi - 1:
-                rot = work.tile([P, width], F32, name="rot")
-                adder.tensor_tensor(out=rot[:], in0=a_cos[:], in1=a_sin[:], op=ADD)
-                q_hi = min(hi, Q_BLOCKS)
-                if lo < q_hi:
-                    nc.sync.dma_start(
-                        out=out_0[0, HEADS_BLK * lo:HEADS_BLK * q_hi, tok, :].rearrange("h p d -> p h d"),
-                        in_=by_head(rot[:, 0:(q_hi - lo) * BLK]),
-                    )
-                if hi > Q_BLOCKS:
-                    nc.sync.dma_start(
-                        out=out_1[0, :, tok, :].rearrange("h p d -> p h d"),
-                        in_=by_head(rot[:, (Q_BLOCKS - lo) * BLK:width]),
-                    )
+                if i == UNITS - 1:
+                    deferred.append((i, lo, hi, adder, a_cos, a_sin))
+                else:
+                    add_and_store(i, lo, hi, adder, a_cos, a_sin)
+            if i == UNITS - 1 and n == QK_BLOCKS - 1:
+                for item in deferred:
+                    add_and_store(*item)

@@ -26,11 +26,10 @@ Q_BLOCKS = H * HD // BLK
 FLOPS = 2 * T * D * N_ALL
 
 X_CODE_CHUNKS = ((0, 2), (2, 2), (4, 4), (8, 6), (14, 6))
-X_SCALE_CHUNKS = ((0, 2), (2, 18))
-W_SCALE_CHUNKS = ((0, 1), (1, 2), (3, 3))
-TABLE_CHUNKS = ((0, 2), (2, 4), (6, 14))
+X_SCALE_CHUNKS = ((0, 4), (4, 16))
+W_SCALE_CHUNKS = ((0, 2), (2, 4))
+TABLE_CHUNKS = ((0, 2), (2, 18))
 HELD_V_UNITS = 4
-WARM_MATMULS = 16
 
 
 def chunk_lookup(chunks):
@@ -64,7 +63,7 @@ def tile_fusedqkvattentionwrapper_pa_kernel(
     with ExitStack() as ctx:
         ctx.enter_context(tc.manual_schedule())
         keep = ctx.enter_context(tc.tile_pool(name="keep", bufs=1))
-        work = ctx.enter_context(tc.tile_pool(name="work", bufs=4))
+        work = ctx.enter_context(tc.tile_pool(name="work", bufs=5))
         vals = ctx.enter_context(tc.tile_pool(name="vals", bufs=4))
         psum = ctx.enter_context(tc.psum_pool(name="psum", bufs=8))
 
@@ -114,80 +113,51 @@ def tile_fusedqkvattentionwrapper_pa_kernel(
             st, cnt = W_SCALE_CHUNKS[c]
             load_scales(ws[c], w_qkv_scales, BLK * st, BLK * (st + cnt))
 
-        def load_angles(c, queue):
-            st, cnt = TABLE_CHUNKS[c]
-            rows = slice(P * st, P * (st + cnt))
-            queue.dma_start(out=cos_raw[c][:], in_=freqs_cos[rows, :].rearrange("(i p) j -> p i j", p=P))
-            queue.dma_start(out=sin_raw[c][:], in_=freqs_sin[rows, :].rearrange("(i p) j -> p i j", p=P))
-
-        warm = keep.tile([P, P + BLK], BF16, name="warm")
-        nc.gpsimd.memset(warm[:], 0.0)
-        for plane in (xs[0], ws[0], ws[1], ws[2], xs[1]):
+        for plane in (xs[0], ws[0], ws[1], xs[1]):
             nc.vector.memset(plane[:].bitcast(I32), 0)
 
-        load_angles(0, nc.gpsimd)
+        for c, (st, cnt) in enumerate(TABLE_CHUNKS):
+            rows = slice(P * st, P * (st + cnt))
+            nc.gpsimd.dma_start(out=cos_raw[c][:], in_=freqs_cos[rows, :].rearrange("(i p) j -> p i j", p=P))
+            nc.gpsimd.dma_start(out=sin_raw[c][:], in_=freqs_sin[rows, :].rearrange("(i p) j -> p i j", p=P))
+
         load_x_codes(0)
         load_w_codes(0)
         load_x_scales(0)
         load_w_scales(0)
         load_w_codes(1)
-        load_w_scales(1)
         load_w_codes(2)
+        load_w_scales(1)
         load_w_codes(3)
-        load_w_scales(2)
         load_w_codes(4)
         load_w_codes(5)
-        load_angles(1, nc.sync)
         load_x_codes(1)
-        load_x_scales(1)
         load_x_codes(2)
-        load_angles(2, nc.sync)
+        load_x_scales(1)
         load_x_codes(3)
         load_x_codes(4)
 
-        warm_acc = psum.tile([P, BLK], F32, name="acc")
-        for k in range(WARM_MATMULS):
-            nc.tensor.matmul(out=warm_acc[:], lhsT=warm[:, 0:P], rhs=warm[:, P:P + BLK], start=True, stop=True)
-
-        def build_tables(c):
-            st, cnt = TABLE_CHUNKS[c]
+        for c, (st, cnt) in enumerate(TABLE_CHUNKS):
             flat_cos = cos_raw[c][:].rearrange("p i j -> p (i j)")
             flat_sin = sin_raw[c][:].rearrange("p i j -> p (i j)")
             cos_pairs = cos_tab[c][:].rearrange("p i (j t) -> p (i j) t", t=2)
             sin_pairs = sin_tab[c][:].rearrange("p i (j t) -> p (i j) t", t=2)
             nc.scalar.copy(out=cos_pairs, in_=flat_cos.unsqueeze(2).to_broadcast([P, cnt * HALF, 2]))
-            nc.scalar.mul(out=sin_pairs[:, :, 0], in_=flat_sin, mul=-1.0)
-            nc.scalar.copy(out=sin_pairs[:, :, 1], in_=flat_sin)
-
-        build_tables(0)
-        build_tables(1)
+            if c == 0:
+                nc.scalar.mul(out=sin_pairs[:, :, 1], in_=flat_sin, mul=-1.0)
+                nc.scalar.copy(out=sin_pairs[:, :, 0], in_=flat_sin)
+            else:
+                nc.gpsimd.tensor_scalar(out=sin_pairs[:, :, 1], in0=flat_sin, scalar1=-1.0, scalar2=0.0,
+                                        op0=MULT, op1=ADD)
+                nc.gpsimd.tensor_scalar(out=sin_pairs[:, :, 0], in0=flat_sin, scalar1=1.0, scalar2=0.0,
+                                        op0=MULT, op1=ADD)
 
         def chunks_of(i):
             if i == UNITS - 1:
-                return ((0, 2, nc.vector), (2, 4, nc.vector), (4, 5, nc.vector))
-            if i < 2:
-                return ((0, 3, nc.gpsimd), (3, 5, nc.gpsimd))
-            return ((0, 5, nc.gpsimd),)
+                return ((0, 3, nc.gpsimd), (3, 5, nc.vector))
+            return ((0, 3, nc.gpsimd), (3, 5, nc.gpsimd))
 
         live = {}
-        deferred = []
-
-        def add_and_store(i, lo, hi, adder, a_cos, a_sin):
-            tok = slice(P * i, P * (i + 1))
-            width = (hi - lo) * BLK
-            rot = work.tile([P, width], F32, name="rot")
-            adder.tensor_tensor(out=rot[:], in0=a_cos[:], in1=a_sin[:], op=ADD)
-            q_hi = min(hi, Q_BLOCKS)
-            if lo < q_hi:
-                nc.sync.dma_start(
-                    out=out_0[0, HEADS_BLK * lo:HEADS_BLK * q_hi, tok, :].rearrange("h p d -> p h d"),
-                    in_=by_head(rot[:, 0:(q_hi - lo) * BLK]),
-                )
-            if hi > Q_BLOCKS:
-                nc.sync.dma_start(
-                    out=out_1[0, :, tok, :].rearrange("h p d -> p h d"),
-                    in_=by_head(rot[:, (Q_BLOCKS - lo) * BLK:width]),
-                )
 
         def by_head(ap):
             return ap.rearrange("p (h d) -> p h d", d=HD)
@@ -216,8 +186,6 @@ def tile_fusedqkvattentionwrapper_pa_kernel(
                 v_sb = vals.tile([P, BLK], F32, name="v_sb")
                 nc.scalar.copy(out=v_sb[:], in_=acc[:])
                 nc.scalar.dma_start(out=out_2[0, :, tok, :].rearrange("h p d -> p h d"), in_=by_head(v_sb[:]))
-                if i == 1:
-                    build_tables(2)
                 continue
 
             lo, hi, adder = [ch for ch in chunks_of(i) if ch[0] <= n < ch[1]][0]
@@ -225,8 +193,9 @@ def tile_fusedqkvattentionwrapper_pa_kernel(
             if n == lo:
                 a_cos = work.tile([P, width], F32, name="a_cos")
                 a_sin = work.tile([P, width], F32, name="a_sin")
-                live[i] = (a_cos, a_sin)
-            a_cos, a_sin = live[i]
+                a_swp = work.tile([P, width], F32, name="a_swp")
+                live[i] = (a_cos, a_sin, a_swp)
+            a_cos, a_sin, a_swp = live[i]
             cols = slice((n - lo) * BLK, (n - lo + 1) * BLK)
             tcn, tk = tab_of[i]
             shape4 = [P, HEADS_BLK, HALF, 2]
@@ -234,13 +203,20 @@ def tile_fusedqkvattentionwrapper_pa_kernel(
             sin_v = sin_tab[tcn][:, tk, :].rearrange("p (j t) -> p j t", t=2).unsqueeze(1).to_broadcast(shape4)
             pairs = by_pair(acc[:])
             nc.vector.tensor_tensor(out=by_pair(a_cos[:, cols]), in0=pairs, in1=cos_v, op=MULT)
-            nc.vector.tensor_tensor(out=by_pair(a_sin[:, cols]), in0=pairs[:, :, :, ::-1], in1=sin_v, op=MULT)
+            nc.vector.tensor_tensor(out=by_pair(a_sin[:, cols]), in0=pairs, in1=sin_v, op=MULT)
+            nc.scalar.copy(out=by_pair(a_swp[:, cols]), in_=by_pair(a_sin[:, cols])[:, :, :, ::-1])
 
             if n == hi - 1:
-                if i == UNITS - 1:
-                    deferred.append((i, lo, hi, adder, a_cos, a_sin))
-                else:
-                    add_and_store(i, lo, hi, adder, a_cos, a_sin)
-            if i == UNITS - 1 and n == QK_BLOCKS - 1:
-                for item in deferred:
-                    add_and_store(*item)
+                rot = work.tile([P, width], F32, name="rot")
+                adder.tensor_tensor(out=rot[:], in0=a_cos[:], in1=a_swp[:], op=ADD)
+                q_hi = min(hi, Q_BLOCKS)
+                if lo < q_hi:
+                    nc.sync.dma_start(
+                        out=out_0[0, HEADS_BLK * lo:HEADS_BLK * q_hi, tok, :].rearrange("h p d -> p h d"),
+                        in_=by_head(rot[:, 0:(q_hi - lo) * BLK]),
+                    )
+                if hi > Q_BLOCKS:
+                    nc.sync.dma_start(
+                        out=out_1[0, :, tok, :].rearrange("h p d -> p h d"),
+                        in_=by_head(rot[:, (Q_BLOCKS - lo) * BLK:width]),
+                    )

@@ -27,9 +27,11 @@ FLOPS = 2 * T * D * N_ALL
 
 X_CODE_CHUNKS = ((0, 2), (2, 2), (4, 4), (8, 6), (14, 6))
 X_SCALE_CHUNKS = ((0, 4), (4, 16))
-W_SCALE_CHUNKS = ((0, 2), (2, 4))
-TABLE_CHUNKS = ((0, 2), (2, 18))
+W_SCALE_CHUNKS = ((5, 1), (0, 1), (1, 2), (3, 2))
+TABLE_CHUNKS = ((0, 4), (4, 4), (8, 12))
+HEAD_UNITS = 4
 HELD_V_UNITS = 4
+WARM_MATMULS = 12
 
 
 def chunk_lookup(chunks):
@@ -42,10 +44,10 @@ def chunk_lookup(chunks):
 
 def job_order():
     jobs = []
-    for n in range(QK_BLOCKS + 1):
-        for i in (0, 1):
+    for n in [V_BLOCK] + list(range(QK_BLOCKS)):
+        for i in range(HEAD_UNITS):
             jobs.append((i, n))
-    for i in range(2, UNITS - HELD_V_UNITS):
+    for i in range(HEAD_UNITS, UNITS - HELD_V_UNITS):
         for n in range(QK_BLOCKS + 1):
             jobs.append((i, n))
     for i in range(UNITS - HELD_V_UNITS, UNITS):
@@ -63,7 +65,7 @@ def tile_fusedqkvattentionwrapper_pa_kernel(
     with ExitStack() as ctx:
         ctx.enter_context(tc.manual_schedule())
         keep = ctx.enter_context(tc.tile_pool(name="keep", bufs=1))
-        work = ctx.enter_context(tc.tile_pool(name="work", bufs=5))
+        work = ctx.enter_context(tc.tile_pool(name="work", bufs=7))
         vals = ctx.enter_context(tc.tile_pool(name="vals", bufs=4))
         psum = ctx.enter_context(tc.psum_pool(name="psum", bufs=8))
 
@@ -99,10 +101,10 @@ def tile_fusedqkvattentionwrapper_pa_kernel(
             )
 
         def load_scales(plane, dram, lo, hi):
-            for q in range(4):
+            for r in range(4):
                 nc.sync.dma_start(
-                    out=plane[32 * q:32 * q + 4, :, :].bitcast(I32),
-                    in_=dram[:, 4 * q:4 * q + 4, lo:hi].rearrange("g r n -> r g n").bitcast(I32),
+                    out=plane[r:P:32, :, :].bitcast(I32),
+                    in_=dram[:, r:16:4, lo:hi].rearrange("g q n -> q g n").bitcast(I32),
                 )
 
         def load_x_scales(c):
@@ -113,46 +115,66 @@ def tile_fusedqkvattentionwrapper_pa_kernel(
             st, cnt = W_SCALE_CHUNKS[c]
             load_scales(ws[c], w_qkv_scales, BLK * st, BLK * (st + cnt))
 
-        for plane in (xs[0], ws[0], ws[1], xs[1]):
+        def load_angles(c, queue):
+            st, cnt = TABLE_CHUNKS[c]
+            rows = slice(P * st, P * (st + cnt))
+            queue.dma_start(out=cos_raw[c][:], in_=freqs_cos[rows, :].rearrange("(i p) j -> p i j", p=P))
+            queue.dma_start(out=sin_raw[c][:], in_=freqs_sin[rows, :].rearrange("(i p) j -> p i j", p=P))
+
+        warm = keep.tile([P, P + BLK], BF16, name="warm")
+        nc.gpsimd.memset(warm[:], 0.0)
+        first_act = keep.tile([P, 1], F32, name="first_act")
+        nc.scalar.copy(out=first_act[:], in_=warm[:, 0:1])
+        for plane in (xs[0], ws[0], ws[1], ws[2], ws[3], xs[1]):
             nc.vector.memset(plane[:].bitcast(I32), 0)
 
-        for c, (st, cnt) in enumerate(TABLE_CHUNKS):
-            rows = slice(P * st, P * (st + cnt))
-            nc.gpsimd.dma_start(out=cos_raw[c][:], in_=freqs_cos[rows, :].rearrange("(i p) j -> p i j", p=P))
-            nc.gpsimd.dma_start(out=sin_raw[c][:], in_=freqs_sin[rows, :].rearrange("(i p) j -> p i j", p=P))
-
         load_x_codes(0)
-        load_w_codes(0)
+        load_w_codes(V_BLOCK)
         load_x_scales(0)
         load_w_scales(0)
-        load_w_codes(1)
-        load_w_codes(2)
-        load_w_scales(1)
-        load_w_codes(3)
-        load_w_codes(4)
-        load_w_codes(5)
         load_x_codes(1)
+        load_angles(0, nc.sync)
+        load_w_codes(0)
+        load_w_scales(1)
+        load_w_codes(1)
+        load_w_scales(2)
+        load_w_codes(2)
+        load_w_codes(3)
+        load_w_scales(3)
+        load_w_codes(4)
+        load_angles(1, nc.sync)
         load_x_codes(2)
         load_x_scales(1)
-        load_x_codes(3)
-        load_x_codes(4)
 
-        for c, (st, cnt) in enumerate(TABLE_CHUNKS):
+        warm_acc = psum.tile([P, BLK], F32, name="acc")
+        for k in range(WARM_MATMULS):
+            nc.tensor.matmul(out=warm_acc[:], lhsT=warm[:, 0:P], rhs=warm[:, P:P + BLK], start=True, stop=True)
+
+        def build_tables(c):
+            st, cnt = TABLE_CHUNKS[c]
             flat_cos = cos_raw[c][:].rearrange("p i j -> p (i j)")
             flat_sin = sin_raw[c][:].rearrange("p i j -> p (i j)")
             cos_pairs = cos_tab[c][:].rearrange("p i (j t) -> p (i j) t", t=2)
             sin_pairs = sin_tab[c][:].rearrange("p i (j t) -> p (i j) t", t=2)
             nc.scalar.copy(out=cos_pairs, in_=flat_cos.unsqueeze(2).to_broadcast([P, cnt * HALF, 2]))
-            if c == 0:
-                nc.scalar.mul(out=sin_pairs[:, :, 1], in_=flat_sin, mul=-1.0)
-                nc.scalar.copy(out=sin_pairs[:, :, 0], in_=flat_sin)
-            else:
-                nc.gpsimd.tensor_scalar(out=sin_pairs[:, :, 1], in0=flat_sin, scalar1=-1.0, scalar2=0.0,
-                                        op0=MULT, op1=ADD)
-                nc.gpsimd.tensor_scalar(out=sin_pairs[:, :, 0], in0=flat_sin, scalar1=1.0, scalar2=0.0,
-                                        op0=MULT, op1=ADD)
+            nc.scalar.mul(out=sin_pairs[:, :, 0], in_=flat_sin, mul=-1.0)
+            nc.scalar.copy(out=sin_pairs[:, :, 1], in_=flat_sin)
+
+        def late_loads():
+            load_angles(2, nc.sync)
+            load_x_codes(3)
+            load_x_codes(4)
+            build_tables(2)
+
+        after_job = {
+            (1, V_BLOCK): lambda: build_tables(0),
+            (HEAD_UNITS - 1, V_BLOCK): lambda: build_tables(1),
+            (HEAD_UNITS - 1, 1): late_loads,
+        }
 
         def chunks_of(i):
+            if i < HEAD_UNITS:
+                return [(b, b + 1, nc.gpsimd) for b in range(QK_BLOCKS)]
             if i == UNITS - 1:
                 return ((0, 3, nc.gpsimd), (3, 5, nc.vector))
             return ((0, 3, nc.gpsimd), (3, 5, nc.gpsimd))
@@ -186,6 +208,8 @@ def tile_fusedqkvattentionwrapper_pa_kernel(
                 v_sb = vals.tile([P, BLK], F32, name="v_sb")
                 nc.scalar.copy(out=v_sb[:], in_=acc[:])
                 nc.scalar.dma_start(out=out_2[0, :, tok, :].rearrange("h p d -> p h d"), in_=by_head(v_sb[:]))
+                if (i, n) in after_job:
+                    after_job[(i, n)]()
                 continue
 
             lo, hi, adder = [ch for ch in chunks_of(i) if ch[0] <= n < ch[1]][0]
@@ -193,9 +217,8 @@ def tile_fusedqkvattentionwrapper_pa_kernel(
             if n == lo:
                 a_cos = work.tile([P, width], F32, name="a_cos")
                 a_sin = work.tile([P, width], F32, name="a_sin")
-                a_swp = work.tile([P, width], F32, name="a_swp")
-                live[i] = (a_cos, a_sin, a_swp)
-            a_cos, a_sin, a_swp = live[i]
+                live[i] = (a_cos, a_sin)
+            a_cos, a_sin = live[i]
             cols = slice((n - lo) * BLK, (n - lo + 1) * BLK)
             tcn, tk = tab_of[i]
             shape4 = [P, HEADS_BLK, HALF, 2]
@@ -203,12 +226,11 @@ def tile_fusedqkvattentionwrapper_pa_kernel(
             sin_v = sin_tab[tcn][:, tk, :].rearrange("p (j t) -> p j t", t=2).unsqueeze(1).to_broadcast(shape4)
             pairs = by_pair(acc[:])
             nc.vector.tensor_tensor(out=by_pair(a_cos[:, cols]), in0=pairs, in1=cos_v, op=MULT)
-            nc.vector.tensor_tensor(out=by_pair(a_sin[:, cols]), in0=pairs, in1=sin_v, op=MULT)
-            nc.scalar.copy(out=by_pair(a_swp[:, cols]), in_=by_pair(a_sin[:, cols])[:, :, :, ::-1])
+            nc.vector.tensor_tensor(out=by_pair(a_sin[:, cols]), in0=pairs[:, :, :, ::-1], in1=sin_v, op=MULT)
 
             if n == hi - 1:
                 rot = work.tile([P, width], F32, name="rot")
-                adder.tensor_tensor(out=rot[:], in0=a_cos[:], in1=a_swp[:], op=ADD)
+                adder.tensor_tensor(out=rot[:], in0=a_cos[:], in1=a_sin[:], op=ADD)
                 q_hi = min(hi, Q_BLOCKS)
                 if lo < q_hi:
                     nc.sync.dma_start(
@@ -220,3 +242,5 @@ def tile_fusedqkvattentionwrapper_pa_kernel(
                         out=out_1[0, :, tok, :].rearrange("h p d -> p h d"),
                         in_=by_head(rot[:, (Q_BLOCKS - lo) * BLK:width]),
                     )
+            if (i, n) in after_job:
+                after_job[(i, n)]()

@@ -30,7 +30,8 @@ X_SCALE_CHUNKS = ((0, 4), (4, 16))
 W_SCALE_CHUNKS = ((5, 1), (0, 1), (1, 2), (3, 2))
 TABLE_CHUNKS = ((0, 4), (4, 4), (8, 12))
 HEAD_UNITS = 4
-HELD_V_UNITS = 4
+DEFERRED_V_UNITS = (12, 15, 18, 19)
+LAST_UNIT_CHUNKS = ((0, 2), (2, 4), (4, 5))
 WARM_MATMULS = 12
 
 
@@ -47,14 +48,17 @@ def job_order():
     for n in [V_BLOCK] + list(range(QK_BLOCKS)):
         for i in range(HEAD_UNITS):
             jobs.append((i, n))
-    for i in range(HEAD_UNITS, UNITS - HELD_V_UNITS):
-        for n in range(QK_BLOCKS + 1):
-            jobs.append((i, n))
-    for i in range(UNITS - HELD_V_UNITS, UNITS):
+    for i in range(HEAD_UNITS, UNITS - 1):
         for n in range(QK_BLOCKS):
             jobs.append((i, n))
-    for i in range(UNITS - HELD_V_UNITS, UNITS):
-        jobs.append((i, V_BLOCK))
+        if i not in DEFERRED_V_UNITS:
+            jobs.append((i, V_BLOCK))
+    deferred = [(i, V_BLOCK) for i in DEFERRED_V_UNITS]
+    for c, (lo, hi) in enumerate(LAST_UNIT_CHUNKS):
+        for n in range(lo, hi):
+            jobs.append((UNITS - 1, n))
+        jobs.append(deferred[c])
+    jobs.extend(deferred[len(LAST_UNIT_CHUNKS):])
     return jobs
 
 
@@ -176,7 +180,7 @@ def tile_fusedqkvattentionwrapper_pa_kernel(
             if i < HEAD_UNITS:
                 return [(b, b + 1, nc.gpsimd) for b in range(QK_BLOCKS)]
             if i == UNITS - 1:
-                return ((0, 3, nc.gpsimd), (3, 5, nc.vector))
+                return [(lo, hi, nc.vector if hi == QK_BLOCKS else nc.gpsimd) for lo, hi in LAST_UNIT_CHUNKS]
             return ((0, 3, nc.gpsimd), (3, 5, nc.gpsimd))
 
         live = {}

@@ -25,14 +25,14 @@ Q_BLOCKS = H * HD // BLK
 
 FLOPS = 2 * T * D * N_ALL
 
-X_CODE_CHUNKS = ((0, 2), (2, 2), (4, 4), (8, 6), (14, 6))
+X_CODE_CHUNKS = ((0, 1), (1, 3), (4, 4), (8, 6), (14, 6))
 X_SCALE_CHUNKS = ((0, 4), (4, 16))
 W_SCALE_CHUNKS = ((5, 1), (0, 1), (1, 2), (3, 2))
 TABLE_CHUNKS = ((0, 4), (4, 4), (8, 12))
 HEAD_UNITS = 4
 DEFERRED_V_UNITS = (12, 15, 18, 19)
 LAST_UNIT_CHUNKS = ((0, 2), (2, 4), (4, 5))
-WARM_MATMULS = 12
+WARM_MATMULS = 11
 
 
 def chunk_lookup(chunks):
@@ -98,10 +98,10 @@ def tile_fusedqkvattentionwrapper_pa_kernel(
                 in_=x_words[:, :, 2 * P * st:2 * P * (st + cnt)].rearrange("g p n -> p g n").bitcast(I32),
             )
 
-        def load_w_codes(n):
+        def load_w_codes(n, g_lo=0, g_hi=PASSES):
             nc.sync.dma_start(
-                out=ww[n][:].bitcast(I32),
-                in_=w_qkv_words[:, :, 2 * BLK * n:2 * BLK * (n + 1)].rearrange("g p n -> p g n").bitcast(I32),
+                out=ww[n][:, g_lo:g_hi, :].bitcast(I32),
+                in_=w_qkv_words[g_lo:g_hi, :, 2 * BLK * n:2 * BLK * (n + 1)].rearrange("g p n -> p g n").bitcast(I32),
             )
 
         def load_scales(plane, dram, lo, hi):
@@ -133,9 +133,10 @@ def tile_fusedqkvattentionwrapper_pa_kernel(
             nc.vector.memset(plane[:].bitcast(I32), 0)
 
         load_x_codes(0)
-        load_w_codes(V_BLOCK)
+        load_w_codes(V_BLOCK, 0, 2)
         load_x_scales(0)
         load_w_scales(0)
+        load_w_codes(V_BLOCK, 2, PASSES)
         load_x_codes(1)
         load_angles(0, nc.sync)
         load_w_codes(0)

@@ -27,7 +27,7 @@ FLOPS = 2 * T * D * N_ALL
 
 X_CODE_CHUNKS = ((0, 1), (1, 3), (4, 4), (8, 6), (14, 6))
 X_SCALE_CHUNKS = ((0, 4), (4, 16))
-W_SCALE_CHUNKS = ((5, 1), (0, 1), (1, 2), (3, 2))
+W_SCALE_CHUNKS = ((0, 1), (1, 1), (2, 2), (4, 2))
 TABLE_CHUNKS = ((0, 4), (4, 4), (8, 12))
 HEAD_UNITS = 4
 DEFERRED_V_UNITS = (12, 15, 18, 19)
@@ -45,7 +45,7 @@ def chunk_lookup(chunks):
 
 def job_order():
     jobs = []
-    for n in [V_BLOCK] + list(range(QK_BLOCKS)):
+    for n in range(QK_BLOCKS + 1):
         for i in range(HEAD_UNITS):
             jobs.append((i, n))
     for i in range(HEAD_UNITS, UNITS - 1):
@@ -132,21 +132,21 @@ def tile_fusedqkvattentionwrapper_pa_kernel(
         for plane in (xs[0], ws[0], ws[1], ws[2], ws[3], xs[1]):
             nc.vector.memset(plane[:].bitcast(I32), 0)
 
+        load_angles(0, nc.gpsimd)
         load_x_codes(0)
-        load_w_codes(V_BLOCK, 0, 2)
+        load_w_codes(0, 0, 2)
         load_x_scales(0)
         load_w_scales(0)
-        load_w_codes(V_BLOCK, 2, PASSES)
+        load_w_codes(0, 2, PASSES)
         load_x_codes(1)
-        load_angles(0, nc.sync)
-        load_w_codes(0)
-        load_w_scales(1)
         load_w_codes(1)
-        load_w_scales(2)
+        load_w_scales(1)
         load_w_codes(2)
+        load_w_scales(2)
         load_w_codes(3)
-        load_w_scales(3)
         load_w_codes(4)
+        load_w_scales(3)
+        load_w_codes(V_BLOCK)
         load_angles(1, nc.sync)
         load_x_codes(2)
         load_x_scales(1)
@@ -171,11 +171,9 @@ def tile_fusedqkvattentionwrapper_pa_kernel(
             load_x_codes(4)
             build_tables(2)
 
-        after_job = {
-            (1, V_BLOCK): lambda: build_tables(0),
-            (HEAD_UNITS - 1, V_BLOCK): lambda: build_tables(1),
-            (HEAD_UNITS - 1, 1): late_loads,
-        }
+        build_tables(0)
+        build_tables(1)
+        after_job = {(HEAD_UNITS - 1, 1): late_loads}
 
         def chunks_of(i):
             if i < HEAD_UNITS:

@@ -30,7 +30,8 @@ X_SCALE_CHUNKS = ((0, 4), (4, 16))
 W_SCALE_CHUNKS = ((0, 1), (1, 1), (2, 2), (4, 2))
 TABLE_CHUNKS = ((0, 4), (4, 4), (8, 12))
 HEAD_UNITS = 4
-DEFERRED_V_UNITS = (12, 15, 18, 19)
+DEFERRED_V_UNITS = (6, 9, 12, 15, 18, 19)
+VALUE_JOBS_BEHIND_CHUNK = (2, 2, 2)
 LAST_UNIT_CHUNKS = ((0, 2), (2, 4), (4, 5))
 WARM_MATMULS = 11
 
@@ -54,11 +55,12 @@ def job_order():
         if i not in DEFERRED_V_UNITS:
             jobs.append((i, V_BLOCK))
     deferred = [(i, V_BLOCK) for i in DEFERRED_V_UNITS]
-    for c, (lo, hi) in enumerate(LAST_UNIT_CHUNKS):
+    for (lo, hi), count in zip(LAST_UNIT_CHUNKS, VALUE_JOBS_BEHIND_CHUNK):
         for n in range(lo, hi):
             jobs.append((UNITS - 1, n))
-        jobs.append(deferred[c])
-    jobs.extend(deferred[len(LAST_UNIT_CHUNKS):])
+        jobs.extend(deferred[:count])
+        deferred = deferred[count:]
+    assert not deferred
     return jobs
 
 

@@ -75,14 +75,18 @@ def tile_fusedqkvattentionwrapper_pa_kernel(
         vals = ctx.enter_context(tc.tile_pool(name="vals", bufs=4))
         psum = ctx.enter_context(tc.psum_pool(name="psum", bufs=8))
 
-        xw = [keep.tile([P, PASSES, 2 * P * cnt], U8, name="xw%d" % c, align_bytes=64)
-              for c, (st, cnt) in enumerate(X_CODE_CHUNKS)]
-        xs = [keep.tile([P, PASSES, P * cnt], U8, name="xs%d" % c, align_bytes=64)
-              for c, (st, cnt) in enumerate(X_SCALE_CHUNKS)]
-        ww = [keep.tile([P, PASSES, 2 * BLK], U8, name="ww%d" % n, align_bytes=64)
-              for n in range(QK_BLOCKS + 1)]
-        ws = [keep.tile([P, PASSES, BLK * cnt], U8, name="ws%d" % c, align_bytes=64)
-              for c, (st, cnt) in enumerate(W_SCALE_CHUNKS)]
+        operands = ctx.enter_context(tc.tile_pool(name="operands", bufs=1))
+        used = [0]
+
+        def operand_tile(width, name, phase):
+            start = used[0] + (phase - used[0]) % 256
+            used[0] = start + PASSES * width
+            return operands.tile([P, PASSES, width], U8, name=name, align_bytes=256 if start == 0 else 64, offset=start)
+
+        ww = [operand_tile(2 * BLK, "ww%d" % n, 0) for n in range(QK_BLOCKS + 1)]
+        ws = [operand_tile(BLK * cnt, "ws%d" % c, 128) for c, (st, cnt) in enumerate(W_SCALE_CHUNKS)]
+        xw = [operand_tile(2 * P * cnt, "xw%d" % c, 64) for c, (st, cnt) in enumerate(X_CODE_CHUNKS)]
+        xs = [operand_tile(P * cnt, "xs%d" % c, 192) for c, (st, cnt) in enumerate(X_SCALE_CHUNKS)]
         cos_raw = [keep.tile([P, cnt, HALF], BF16, name="cosr%d" % c) for c, (st, cnt) in enumerate(TABLE_CHUNKS)]
         sin_raw = [keep.tile([P, cnt, HALF], BF16, name="sinr%d" % c) for c, (st, cnt) in enumerate(TABLE_CHUNKS)]
         cos_tab = [keep.tile([P, cnt, HD], F32, name="cost%d" % c) for c, (st, cnt) in enumerate(TABLE_CHUNKS)]

@@ -31,7 +31,7 @@ W_SCALE_CHUNKS = ((0, 1), (1, 1), (2, 2), (4, 2))
 TABLE_CHUNKS = ((0, 4), (4, 4), (8, 12))
 HEAD_UNITS = 4
 DEFERRED_V_UNITS = (6, 9, 12, 15, 18, 19)
-VALUE_JOBS_BEHIND_CHUNK = (2, 2, 2)
+VALUE_JOBS_BEHIND_CHUNK = (1, 2, 3)
 LAST_UNIT_CHUNKS = ((0, 2), (2, 4), (4, 5))
 WARM_MATMULS = 11
 

@@ -30,8 +30,8 @@ X_SCALE_CHUNKS = ((0, 4), (4, 16))
 W_SCALE_CHUNKS = ((0, 1), (1, 1), (2, 2), (4, 2))
 TABLE_CHUNKS = ((0, 4), (4, 4), (8, 12))
 HEAD_UNITS = 4
-DEFERRED_V_UNITS = (6, 9, 12, 15, 18, 19)
-VALUE_JOBS_BEHIND_CHUNK = (1, 2, 3)
+DEFERRED_V_UNITS = (0, 1, 2, 3, 4, 19)
+VALUE_JOBS_BEHIND_CHUNK = (0, 0, 6)
 LAST_UNIT_CHUNKS = ((0, 2), (2, 4), (4, 5))
 WARM_MATMULS = 11
 
@@ -46,7 +46,7 @@ def chunk_lookup(chunks):
 
 def job_order():
     jobs = []
-    for n in range(QK_BLOCKS + 1):
+    for n in range(QK_BLOCKS):
         for i in range(HEAD_UNITS):
             jobs.append((i, n))
     for i in range(HEAD_UNITS, UNITS - 1):
@@ -72,7 +72,7 @@ def tile_fusedqkvattentionwrapper_pa_kernel(
         ctx.enter_context(tc.manual_schedule())
         keep = ctx.enter_context(tc.tile_pool(name="keep", bufs=1))
         work = ctx.enter_context(tc.tile_pool(name="work", bufs=7))
-        vals = ctx.enter_context(tc.tile_pool(name="vals", bufs=4))
+        vals = ctx.enter_context(tc.tile_pool(name="vals", bufs=8))
         psum = ctx.enter_context(tc.psum_pool(name="psum", bufs=8))
 
         operands = ctx.enter_context(tc.tile_pool(name="operands", bufs=1))

from contextlib import ExitStack

import concourse.mybir as mybir

F32 = mybir.dt.float32
BF16 = mybir.dt.bfloat16
I32 = mybir.dt.int32
U8 = mybir.dt.uint8
FP4X4 = mybir.dt.float4_e2m1fn_x4
MULT = mybir.AluOpType.mult
ADD = mybir.AluOpType.add

T, D = 2560, 2048
H, KV, HD = 16, 4, 128
HALF = HD // 2
N_ALL = (H + 2 * KV) * HD
P = 128
PASSES = D // 512
UNITS = T // P
BLK = 512
HEADS_BLK = BLK // HD
QK_BLOCKS = (H + KV) * HD // BLK
V_BLOCK = QK_BLOCKS
Q_BLOCKS = H * HD // BLK

FLOPS = 2 * T * D * N_ALL

X_CODE_CHUNKS = ((0, 1), (1, 3), (4, 4), (8, 6), (14, 6))
X_SCALE_CHUNKS = ((0, 4), (4, 16))
W_SCALE_CHUNKS = ((0, 1), (1, 1), (2, 2), (4, 2))
TABLE_CHUNKS = ((0, 4), (4, 4), (8, 12))
HEAD_UNITS = 4
DEFERRED_V_UNITS = (0, 1, 2, 3, 4, 19)
VALUE_JOBS_BEHIND_CHUNK = (0, 0, 6)
LAST_UNIT_CHUNKS = ((0, 2), (2, 4), (4, 5))
WARM_MATMULS = 11


def chunk_lookup(chunks):
    table = {}
    for c, (start, count) in enumerate(chunks):
        for k in range(count):
            table[start + k] = (c, k)
    return table


def job_order():
    jobs = []
    for n in range(QK_BLOCKS):
        for i in range(HEAD_UNITS):
            jobs.append((i, n))
    for i in range(HEAD_UNITS, UNITS - 1):
        for n in range(QK_BLOCKS):
            jobs.append((i, n))
        if i not in DEFERRED_V_UNITS:
            jobs.append((i, V_BLOCK))
    deferred = [(i, V_BLOCK) for i in DEFERRED_V_UNITS]
    for (lo, hi), count in zip(LAST_UNIT_CHUNKS, VALUE_JOBS_BEHIND_CHUNK):
        for n in range(lo, hi):
            jobs.append((UNITS - 1, n))
        jobs.extend(deferred[:count])
        deferred = deferred[count:]
    assert not deferred
    return jobs


def tile_fusedqkvattentionwrapper_pa_kernel(
    tc, x_words, x_scales, freqs_cos, freqs_sin, w_qkv_words, w_qkv_scales, out_0, out_1, out_2
):
    nc = tc.nc
    with ExitStack() as ctx:
        ctx.enter_context(tc.manual_schedule())
        keep = ctx.enter_context(tc.tile_pool(name="keep", bufs=1))
        work = ctx.enter_context(tc.tile_pool(name="work", bufs=7))
        vals = ctx.enter_context(tc.tile_pool(name="vals", bufs=8))
        psum = ctx.enter_context(tc.psum_pool(name="psum", bufs=8))

        operands = ctx.enter_context(tc.tile_pool(name="operands", bufs=1))
        used = [0]

        def operand_tile(width, name, phase):
            start = used[0] + (phase - used[0]) % 256
            used[0] = start + PASSES * width
            return operands.tile([P, PASSES, width], U8, name=name, align_bytes=256 if start == 0 else 64, offset=start)

        ww = [operand_tile(2 * BLK, "ww%d" % n, 0) for n in range(QK_BLOCKS + 1)]
        ws = [operand_tile(BLK * cnt, "ws%d" % c, 128) for c, (st, cnt) in enumerate(W_SCALE_CHUNKS)]
        xw = [operand_tile(2 * P * cnt, "xw%d" % c, 64) for c, (st, cnt) in enumerate(X_CODE_CHUNKS)]
        xs = [operand_tile(P * cnt, "xs%d" % c, 192) for c, (st, cnt) in enumerate(X_SCALE_CHUNKS)]
        cos_raw = [keep.tile([P, cnt, HALF], BF16, name="cosr%d" % c) for c, (st, cnt) in enumerate(TABLE_CHUNKS)]
        sin_raw = [keep.tile([P, cnt, HALF], BF16, name="sinr%d" % c) for c, (st, cnt) in enumerate(TABLE_CHUNKS)]
        cos_tab = [keep.tile([P, cnt, HD], F32, name="cost%d" % c) for c, (st, cnt) in enumerate(TABLE_CHUNKS)]
        sin_tab = [keep.tile([P, cnt, HD], F32, name="sint%d" % c) for c, (st, cnt) in enumerate(TABLE_CHUNKS)]

        xw_of = chunk_lookup(X_CODE_CHUNKS)
        xs_of = chunk_lookup(X_SCALE_CHUNKS)
        ws_of = chunk_lookup(W_SCALE_CHUNKS)
        tab_of = chunk_lookup(TABLE_CHUNKS)

        def load_x_codes(c):
            st, cnt = X_CODE_CHUNKS[c]
            nc.sync.dma_start(
                out=xw[c][:].bitcast(I32),
                in_=x_words[:, :, 2 * P * st:2 * P * (st + cnt)].rearrange("g p n -> p g n").bitcast(I32),
            )

        def load_w_codes(n, g_lo=0, g_hi=PASSES):
            nc.sync.dma_start(
                out=ww[n][:, g_lo:g_hi, :].bitcast(I32),
                in_=w_qkv_words[g_lo:g_hi, :, 2 * BLK * n:2 * BLK * (n + 1)].rearrange("g p n -> p g n").bitcast(I32),
            )

        def load_scales(plane, dram, lo, hi):
            for r in range(4):
                nc.sync.dma_start(
                    out=plane[r:P:32, :, :].bitcast(I32),
                    in_=dram[:, r:16:4, lo:hi].rearrange("g q n -> q g n").bitcast(I32),
                )

        def load_x_scales(c):
            st, cnt = X_SCALE_CHUNKS[c]
            load_scales(xs[c], x_scales, P * st, P * (st + cnt))

        def load_w_scales(c):
            st, cnt = W_SCALE_CHUNKS[c]
            load_scales(ws[c], w_qkv_scales, BLK * st, BLK * (st + cnt))

        def load_angles(c, queue):
            st, cnt = TABLE_CHUNKS[c]
            rows = slice(P * st, P * (st + cnt))
            queue.dma_start(out=cos_raw[c][:], in_=freqs_cos[rows, :].rearrange("(i p) j -> p i j", p=P))
            queue.dma_start(out=sin_raw[c][:], in_=freqs_sin[rows, :].rearrange("(i p) j -> p i j", p=P))

        warm = keep.tile([P, P + BLK], BF16, name="warm")
        nc.gpsimd.memset(warm[:], 0.0)
        first_act = keep.tile([P, 1], F32, name="first_act")
        nc.scalar.copy(out=first_act[:], in_=warm[:, 0:1])
        for plane in (xs[0], ws[0], ws[1], ws[2], ws[3], xs[1]):
            nc.vector.memset(plane[:].bitcast(I32), 0)

        load_angles(0, nc.gpsimd)
        load_x_codes(0)
        load_w_codes(0, 0, 2)
        load_x_scales(0)
        load_w_scales(0)
        load_w_codes(0, 2, PASSES)
        load_x_codes(1)
        load_w_codes(1)
        load_w_scales(1)
        load_w_codes(2)
        load_w_scales(2)
        load_w_codes(3)
        load_w_codes(4)
        load_w_scales(3)
        load_w_codes(V_BLOCK)
        load_angles(1, nc.sync)
        load_x_codes(2)
        load_x_scales(1)

        warm_acc = psum.tile([P, BLK], F32, name="acc")
        for k in range(WARM_MATMULS):
            nc.tensor.matmul(out=warm_acc[:], lhsT=warm[:, 0:P], rhs=warm[:, P:P + BLK], start=True, stop=True)

        def build_tables(c):
            st, cnt = TABLE_CHUNKS[c]
            flat_cos = cos_raw[c][:].rearrange("p i j -> p (i j)")
            flat_sin = sin_raw[c][:].rearrange("p i j -> p (i j)")
            cos_pairs = cos_tab[c][:].rearrange("p i (j t) -> p (i j) t", t=2)
            sin_pairs = sin_tab[c][:].rearrange("p i (j t) -> p (i j) t", t=2)
            nc.scalar.copy(out=cos_pairs, in_=flat_cos.unsqueeze(2).to_broadcast([P, cnt * HALF, 2]))
            nc.scalar.mul(out=sin_pairs[:, :, 0], in_=flat_sin, mul=-1.0)
            nc.scalar.copy(out=sin_pairs[:, :, 1], in_=flat_sin)

        def late_loads():
            load_angles(2, nc.sync)
            load_x_codes(3)
            load_x_codes(4)
            build_tables(2)

        build_tables(0)
        build_tables(1)
        after_job = {(HEAD_UNITS - 1, 1): late_loads}

        def chunks_of(i):
            if i < HEAD_UNITS:
                return [(b, b + 1, nc.gpsimd) for b in range(QK_BLOCKS)]
            if i == UNITS - 1:
                return [(lo, hi, nc.vector if hi == QK_BLOCKS else nc.gpsimd) for lo, hi in LAST_UNIT_CHUNKS]
            return ((0, 3, nc.gpsimd), (3, 5, nc.gpsimd))

        live = {}

        def by_head(ap):
            return ap.rearrange("p (h d) -> p h d", d=HD)

        def by_pair(ap):
            return ap.rearrange("p (h j t) -> p h j t", j=HALF, t=2)

        for i, n in job_order():
            tok = slice(P * i, P * (i + 1))
            xc, xk = xw_of[i]
            sc, sk = xs_of[i]
            wc, wk = ws_of[n]
            acc = psum.tile([P, BLK], F32, name="acc")
            for g in range(PASSES):
                nc.tensor.matmul_mx(
                    out=acc[:],
                    lhsT=xw[xc][:, g, 2 * P * xk:2 * P * (xk + 1)].bitcast(FP4X4),
                    lhsT_scale=xs[sc][:, g, P * sk:P * (sk + 1)],
                    rhs=ww[n][:, g, :].bitcast(FP4X4),
                    rhs_scale=ws[wc][:, g, BLK * wk:BLK * (wk + 1)],
                    start=(g == 0),
                    stop=(g == PASSES - 1),
                )

            if n == V_BLOCK:
                v_sb = vals.tile([P, BLK], F32, name="v_sb")
                nc.scalar.copy(out=v_sb[:], in_=acc[:])
                nc.scalar.dma_start(out=out_2[0, :, tok, :].rearrange("h p d -> p h d"), in_=by_head(v_sb[:]))
                if (i, n) in after_job:
                    after_job[(i, n)]()
                continue

            lo, hi, adder = [ch for ch in chunks_of(i) if ch[0] <= n < ch[1]][0]
            width = (hi - lo) * BLK
            if n == lo:
                a_cos = work.tile([P, width], F32, name="a_cos")
                a_sin = work.tile([P, width], F32, name="a_sin")
                live[i] = (a_cos, a_sin)
            a_cos, a_sin = live[i]
            cols = slice((n - lo) * BLK, (n - lo + 1) * BLK)
            tcn, tk = tab_of[i]
            shape4 = [P, HEADS_BLK, HALF, 2]
            cos_v = cos_tab[tcn][:, tk, :].rearrange("p (j t) -> p j t", t=2).unsqueeze(1).to_broadcast(shape4)
            sin_v = sin_tab[tcn][:, tk, :].rearrange("p (j t) -> p j t", t=2).unsqueeze(1).to_broadcast(shape4)
            pairs = by_pair(acc[:])
            nc.vector.tensor_tensor(out=by_pair(a_cos[:, cols]), in0=pairs, in1=cos_v, op=MULT)
            nc.vector.tensor_tensor(out=by_pair(a_sin[:, cols]), in0=pairs[:, :, :, ::-1], in1=sin_v, op=MULT)

            if n == hi - 1:
                rot = work.tile([P, width], F32, name="rot")
                adder.tensor_tensor(out=rot[:], in0=a_cos[:], in1=a_sin[:], op=ADD)
                q_hi = min(hi, Q_BLOCKS)
                if lo < q_hi:
                    nc.sync.dma_start(
                        out=out_0[0, HEADS_BLK * lo:HEADS_BLK * q_hi, tok, :].rearrange("h p d -> p h d"),
                        in_=by_head(rot[:, 0:(q_hi - lo) * BLK]),
                    )
                if hi > Q_BLOCKS:
                    nc.sync.dma_start(
                        out=out_1[0, :, tok, :].rearrange("h p d -> p h d"),
                        in_=by_head(rot[:, (Q_BLOCKS - lo) * BLK:width]),
                    )
            if (i, n) in after_job:
                after_job[(i, n)]()
